import numpy as np
import ml_dtypes


def mxq(x, axis, fmt="e4m3"):
    dtype, down = {"e4m3": (ml_dtypes.float8_e4m3fn, 7), "e5m2": (ml_dtypes.float8_e5m2, 14)}[fmt]
    v = np.moveaxis(np.asarray(x, np.float32).astype(ml_dtypes.bfloat16).astype(np.float64), axis, -1)
    blocks = v.reshape(v.shape[:-1] + (-1, 32))
    amax = np.abs(blocks).max(-1, keepdims=True)
    byte = np.maximum(np.where(amax > 0, np.frexp(amax)[1] - 1 + 127, 0) - down, 1)
    scale = np.exp2(byte - 127.0)
    codes = (blocks / scale).astype(np.float32).astype(dtype).astype(np.float64)
    return np.moveaxis((codes * scale).reshape(v.shape), -1, axis)


WIDE = False


def mx_kscale(k):
    if not WIDE:
        return np.ones(k)
    levels = np.array([10, -10, 5, -5, 0])
    if k % 512:
        return np.exp2(np.random.permutation(np.resize(levels, k // 32))).repeat(32)
    a = np.empty((k // 512, 16))
    for p in range(k // 512):
        a[p, :8] = np.random.permutation(np.resize(levels, 8))
        for g in range(8):
            far = levels[np.abs(levels - a[p, g]) >= 10]
            a[p, g + 8] = far[np.random.randint(len(far))]
    return np.exp2(a.ravel()).repeat(32)


BF16 = ml_dtypes.bfloat16


def bf(x):
    return np.asarray(x, np.float32).astype(BF16)


def f64(x):
    return np.asarray(x).astype(np.float64)


B, A, S, F = 512, 16, 256, 512


def setup_inputs():
    s, u = mx_kscale(F), mx_kscale(F)
    t, v = mx_kscale(F), mx_kscale(F)
    return {
        "h1": bf(np.maximum(np.random.standard_normal((B, A, F)) * 1.4, 0.0) * s),
        "W2": bf(np.random.standard_normal((A, F, F)) * 1.4 / np.sqrt(F) / s[:, None] * t),
        "b2": bf(np.random.standard_normal((A, F)) * 0.2 * t),
        "W3": bf(np.random.standard_normal((A, F, S)) / np.sqrt(F) / t[:, None]),
        "b3": bf(np.random.standard_normal((A, S)) * 0.2),
        "g1": bf(np.maximum(np.random.standard_normal((B, F)) * 1.4, 0.0) * u),
        "V2": bf(np.random.standard_normal((F, F)) * 1.4 / np.sqrt(F) / u[:, None] * v),
        "c2": bf(np.random.standard_normal(F) * 0.2 * v),
        "V3": bf(np.random.standard_normal((F, S)) / np.sqrt(F) / v[:, None]),
        "c3": bf(np.random.standard_normal(S) * 0.2),
    }


def reference(h1, W2, b2, W3, b3, g1, V2, c2, V3, c3):
    ha = mxq(f64(h1), 2, "e4m3").transpose(1, 0, 2)
    h2 = np.maximum(f64(bf(ha @ mxq(f64(W2), 1, "e4m3"))) + f64(b2)[:, None, :], 0.0)
    psi_adv = ((mxq(h2, 2, "e4m3") @ mxq(f64(W3), 1, "e4m3")) + f64(b3)[:, None, :]).transpose(1, 0, 2)
    g2 = np.maximum(f64(bf(mxq(f64(g1), 1, "e4m3") @ mxq(f64(V2), 0, "e4m3"))) + f64(c2), 0.0)
    psi_state = (mxq(g2, 1, "e4m3") @ mxq(f64(V3), 0, "e4m3")) + f64(c3)
    return psi_state[:, None, :] + psi_adv - psi_adv.mean(axis=1, keepdims=True)

@@ -1,0 +1,353 @@
+from contextlib import ExitStack
+
+import concourse.mybir as mybir
+from concourse.masks import make_identity
+
+F32 = mybir.dt.float32
+BF16 = mybir.dt.bfloat16
+U32 = mybir.dt.uint32
+U8 = mybir.dt.uint8
+FP8X4 = mybir.dt.float8_e4m3fn_x4
+ACT = mybir.ActivationFunctionType
+ALU = mybir.AluOpType
+AX = mybir.AxisListType
+
+P = 128
+BATCH = 512
+ACTIONS = 16
+S_OUT = 256
+F = 512
+NB = BATCH // P
+LAST = ACTIONS
+BANK_DT = BF16
+MS = 16
+FAST_COPY = True
+
+FLOPS = 2 * (ACTIONS + 1) * BATCH * F * (F + S_OUT)
+
+
+def tile_psicritic_pa_kernel(tc, h1, W2, b2, W3, b3, g1, V2, c2, V3, c3, out):
+    nc = tc.nc
+    with ExitStack() as ctx:
+        keep = ctx.enter_context(tc.tile_pool(name="keep", bufs=1))
+        stream = ctx.enter_context(tc.tile_pool(name="stream", bufs=2))
+        psum = ctx.enter_context(tc.psum_pool(name="psum", bufs=2))
+        ctx.enter_context(tc.manual_schedule())
+
+        ident_f = keep.tile([P, P], F32, name="ident_f")
+        ident_b = keep.tile([P, P], BF16, name="ident_b")
+        brow2 = keep.tile([P, F], BF16, name="brow2")
+        brow3 = keep.tile([P, S_OUT], BF16, name="brow3")
+        b2T = keep.tile([P, 4, LAST + 1], F32, name="b2T")
+        b3T = keep.tile([P, 2, LAST + 1], F32, name="b3T")
+        bsum = keep.tile([P, 2], F32, name="bsum")
+        kb = keep.tile([P, 2], F32, name="kb")
+        warm = keep.tile([P, 1], F32, name="warm")
+        w3q = keep.tile([P, LAST + 1, S_OUT], U32, name="w3q", align_bytes=64)
+        w3s = keep.tile([P, LAST + 1, S_OUT], U8, name="w3s", align_bytes=64)
+        h2q = keep.tile([P, LAST + 1, BATCH], U32, name="h2q", align_bytes=64)
+        h2s = keep.tile([P, LAST + 1, BATCH], U8, name="h2s", align_bytes=64)
+        stT = keep.tile([P, 2, BATCH], F32, name="stT")
+        baseT = keep.tile([P, 2, BATCH], F32, name="baseT")
+
+        t = {}
+
+        def ok(i):
+            return 0 <= i <= LAST
+
+        def load(i):
+            if not ok(i):
+                return
+            x = stream.tile([P, NB, F], BF16, name="x", tag="x", bufs=5)
+            srcx = g1 if i == 0 else h1[:, i - 1, :]
+            nc.sync.dma_start(out=x[:], in_=srcx.rearrange("(b n) k -> n b k", n=P))
+            t["x", i] = x
+            raw2 = stream.tile([P, 4, F], BF16, name="raw2", tag="raw2", bufs=5)
+            src2 = V2 if i == 0 else W2[i - 1, :, :]
+            nc.sync.dma_start(out=raw2[:], in_=src2.rearrange("(p j) c -> p j c", j=4))
+            t["raw2", i] = raw2
+            raw3 = stream.tile([P, 4, S_OUT], BF16, name="raw3", tag="raw3", bufs=5)
+            src3 = V3 if i == 0 else W3[i - 1, :, :]
+            nc.sync.dma_start(out=raw3[:], in_=src3.rearrange("(p j) s -> p j s", j=4))
+            t["raw3", i] = raw3
+
+        def wi2s(i):
+            if not ok(i):
+                return
+            w2g = stream.tile([P, 4 * F], BF16, name="w2g", tag="w2g", bufs=3, align_bytes=64)
+            t["w2g", i] = w2g
+            nc.scalar.copy(
+                out=w2g[:].rearrange("p (t m j) -> p t m j", t=4, j=4)[:, :, P - MS : P, :],
+                in_=t["raw2", i][:].rearrange("p j (m t) -> p t m j", t=4)[:, :, P - MS : P, :],
+            )
+
+        def wi2v(i):
+            if not ok(i):
+                return
+            nc.vector.tensor_copy(
+                out=t["w2g", i][:].rearrange("p (t m j) -> p t m j", t=4, j=4)[:, :, 0 : P - MS, :],
+                in_=t["raw2", i][:].rearrange("p j (m t) -> p t m j", t=4)[:, :, 0 : P - MS, :],
+            )
+
+        def q_w2(i):
+            if not ok(i):
+                return
+            w2c = stream.tile([P, F], U32, name="w2c", tag="w2c", bufs=3, align_bytes=64)
+            w2sc = stream.tile([P, F], U8, name="w2sc", tag="w2sc", bufs=3, align_bytes=64)
+            nc.vector.quantize_mx(out=w2c[:].bitcast(FP8X4), scales=w2sc[:], in_=t["w2g", i][:])
+            t["w2c", i] = w2c
+            t["w2sc", i] = w2sc
+
+        def wa3(i):
+            if not ok(i):
+                return
+            pw = psum.tile([P, 4 * S_OUT], BF16, name="pw", tag="pw", bufs=1)
+            for h in range(2):
+                nc.tensor.matmul(
+                    out=pw[:, 512 * h : 512 * (h + 1)].rearrange("p (s j) -> p s j", j=4),
+                    lhsT=ident_b[:],
+                    rhs=t["raw3", i][:, :, P * h : P * (h + 1)].rearrange("p j s -> p s j"),
+                    start=True,
+                    stop=True,
+                )
+            t["pw", i] = pw
+
+        def w3copy(i):
+            if not ok(i):
+                return
+            w3g = stream.tile([P, 4 * S_OUT], BF16, name="w3g", tag="w3g", bufs=2, align_bytes=64)
+            nc.scalar.copy(out=w3g[:], in_=t["pw", i][:])
+            t["w3g", i] = w3g
+
+        def q_w3(i):
+            if not ok(i):
+                return
+            nc.vector.quantize_mx(
+                out=w3q[:, i, :].bitcast(FP8X4), scales=w3s[:, i, :], in_=t["w3g", i][:]
+            )
+
+        def tr_x(i, hb):
+            if not ok(i):
+                return
+            pt = psum.tile([P, 2, 2, P], F32, name="pt", tag="pt", bufs=2)
+            for bl in range(2):
+                words = t["x", i][:, 2 * hb + bl, :].bitcast(F32)
+                for u in range(2):
+                    nc.tensor.transpose(pt[:, bl, u, :], words[:, u : F // 2 : 2], ident_f[:])
+            t["pt", i, hb] = pt
+
+        def htc(i, hb):
+            if not ok(i):
+                return
+            if hb == 0:
+                xg = stream.tile([P, 4 * BATCH], BF16, name="xg", tag="xg", bufs=2, align_bytes=64)
+                t["xg", i] = xg
+            nc.scalar.copy(
+                out=t["xg", i][:, 1024 * hb : 1024 * (hb + 1)]
+                .bitcast(F32)
+                .rearrange("p (b n u) -> p b n u", b=2, u=2),
+                in_=t["pt", i, hb][:].rearrange("p b u n -> p b n u"),
+            )
+
+        def q_x(i):
+            if not ok(i):
+                return
+            xc = stream.tile([P, BATCH], U32, name="xc", tag="xc", bufs=2, align_bytes=64)
+            xsc = stream.tile([P, BATCH], U8, name="xsc", tag="xsc", bufs=2, align_bytes=64)
+            nc.vector.quantize_mx(out=xc[:].bitcast(FP8X4), scales=xsc[:], in_=t["xg", i][:])
+            t["xc", i] = xc
+            t["xsc", i] = xsc
+
+        def m1(i, tt):
+            if not ok(i):
+                return
+            ps1 = psum.tile([P, BATCH], BANK_DT, name="ps1", tag="ps1", bufs=3)
+            cols = slice(P * tt, P * (tt + 1))
+            nc.tensor.matmul_mx(
+                out=ps1[:],
+                lhsT=t["w2c", i][:, cols].bitcast(FP8X4),
+                lhsT_scale=t["w2sc", i][:, cols],
+                rhs=t["xc", i][:].bitcast(FP8X4),
+                rhs_scale=t["xsc", i][:],
+                start=True,
+                stop=True,
+            )
+            t["ps1", i, tt] = ps1
+
+        def s1a(i, tt):
+            if not ok(i):
+                return
+            row = LAST if i == 0 else i - 1
+            if tt == 0:
+                h2c = stream.tile([P, 4, BATCH], BF16, name="h2c", tag="h2c", bufs=2)
+                t["h2c", i] = h2c
+            nc.scalar.activation(
+                out=t["h2c", i][:, tt, :],
+                in_=t["ps1", i, tt][:],
+                func=ACT.Relu,
+                bias=b2T[:, tt, row : row + 1],
+                scale=1.0,
+            )
+
+        def s1b(i):
+            if not ok(i):
+                return
+            h2g = stream.tile([P, 4 * BATCH], BF16, name="h2g", tag="h2g", bufs=2, align_bytes=64)
+            if FAST_COPY:
+                nc.vector.tensor_copy(
+                    out=h2g[:].rearrange("p (c i j) -> p c j i", i=4, j=4),
+                    in_=t["h2c", i][:].rearrange("p j (c i) -> p c j i", i=4),
+                )
+            else:
+                nc.vector.tensor_copy(
+                    out=h2g[:].rearrange("p (n j) -> p n j", j=4),
+                    in_=t["h2c", i][:].rearrange("p j n -> p n j"),
+                )
+            t["h2g", i] = h2g
+
+        def q_h2(i):
+            if not ok(i):
+                return
+            nc.vector.quantize_mx(
+                out=h2q[:, i, :].bitcast(FP8X4), scales=h2s[:, i, :], in_=t["h2g", i][:]
+            )
+
+        def mm2(dst, i, st, start, stop):
+            cols = slice(P * st, P * (st + 1))
+            nc.tensor.matmul_mx(
+                out=dst,
+                lhsT=w3q[:, i, cols].bitcast(FP8X4),
+                lhsT_scale=w3s[:, i, cols],
+                rhs=h2q[:, i, :].bitcast(FP8X4),
+                rhs_scale=h2s[:, i, :],
+                start=start,
+                stop=stop,
+            )
+
+        def mm_mean(i, st):
+            if not ok(i):
+                return
+            if i <= 1:
+                pm = psum.tile([P, BATCH], F32, name="pm", tag="pm", bufs=2)
+                t["pm", st] = pm
+            mm2(t["pm", st][:], i, st, i <= 1, i == 0 or i == LAST)
+
+        def bias_prep_pe():
+            pb2 = psum.tile([P, 4, P], BF16, name="pb2", tag="pm", bufs=2)
+            for tt in range(4):
+                nc.tensor.transpose(pb2[:, tt, :], brow2[:, tt:F:4], ident_b[:])
+            pb3 = psum.tile([P, 2, P], BF16, name="pb3", tag="pm", bufs=2)
+            for st in range(2):
+                nc.tensor.transpose(pb3[:, st, :], brow3[:, P * st : P * (st + 1)], ident_b[:])
+            t["pb2"] = pb2
+            t["pb3"] = pb3
+
+        def bias_prep_v():
+            nc.vector.tensor_copy(out=b2T[:], in_=t["pb2"][:, :, 0 : LAST + 1])
+            nc.vector.tensor_copy(out=b3T[:], in_=t["pb3"][:, :, 0 : LAST + 1])
+            nc.vector.tensor_reduce(out=bsum[:], in_=b3T[:, :, 0:ACTIONS], axis=AX.X, op=ALU.add)
+            nc.vector.scalar_tensor_tensor(
+                out=kb[:], in0=bsum[:], scalar=-1.0 / ACTIONS, in1=b3T[:, :, ACTIONS],
+                op0=ALU.mult, op1=ALU.add,
+            )
+
+        nc.vector.memset(warm[:], 0.0)
+        nc.vector.memset(brow2[:], 0.0)
+        nc.vector.memset(brow3[:], 0.0)
+        load(0)
+        load(1)
+        make_identity(nc, ident_f[:])
+        make_identity(nc, ident_b[:])
+        nc.scalar.dma_start(out=brow2[0:ACTIONS, :], in_=b2)
+        nc.scalar.dma_start(out=brow2[ACTIONS : ACTIONS + 1, :], in_=c2.rearrange("(o f) -> o f", o=1))
+        nc.scalar.dma_start(out=brow3[0:ACTIONS, :], in_=b3)
+        nc.scalar.dma_start(out=brow3[ACTIONS : ACTIONS + 1, :], in_=c3.rearrange("(o f) -> o f", o=1))
+        nc.scalar.activation(out=warm[:], in_=warm[:], func=ACT.Relu)
+
+        for i in range(-3, LAST + 3):
+            load(i + 5)
+            s1b(i - 1)
+            q_x(i + 1)
+            q_h2(i - 1)
+            s1a(i, 0)
+            m1(i, 3)
+            htc(i + 2, 0)
+            tr_x(i + 3, 0)
+            s1a(i, 1)
+            m1(i + 1, 0)
+            s1a(i, 2)
+            m1(i + 1, 1)
+            htc(i + 2, 1)
+            tr_x(i + 3, 1)
+            s1a(i, 3)
+            m1(i + 1, 2)
+            mm_mean(i - 1, 0)
+            mm_mean(i - 1, 1)
+            w3copy(i + 2)
+            wa3(i + 3)
+            wi2s(i + 3)
+            if i == -2:
+                bias_prep_pe()
+            wi2v(i + 2)
+            q_w3(i + 1)
+            q_w2(i + 2)
+            if i == -2:
+                bias_prep_v()
+            if i == 1:
+                for st in range(2):
+                    nc.vector.tensor_scalar_add(
+                        out=stT[:, st, :], in0=t["pm", st][:], scalar1=kb[:, st : st + 1]
+                    )
+
+        def m2(a):
+            if a >= ACTIONS:
+                return
+            for st in range(2):
+                if a % 2 == 1 and st == 1:
+                    ps2 = psum.tile([P, BATCH], F32, name="ps2", tag="pw", bufs=1)
+                else:
+                    ps2 = psum.tile([P, BATCH], F32, name="ps2", tag="ps1", bufs=3)
+                mm2(ps2[:], a + 1, st, True, True)
+                t["ps2", a, st] = ps2
+
+        for st in range(2):
+            nc.vector.scalar_tensor_tensor(
+                out=baseT[:, st, :], in0=t["pm", st][:], scalar=-1.0 / ACTIONS, in1=stT[:, st, :],
+                op0=ALU.mult, op1=ALU.add,
+            )
+        m2(0)
+        m2(1)
+        for a in range(ACTIONS):
+            advT = stream.tile([P, 2, BATCH], F32, name="advT", tag="advT", bufs=3)
+            for st in range(2):
+                nc.vector.scalar_tensor_tensor(
+                    out=advT[:, st, :], in0=t["ps2", a, st][:], scalar=b3T[:, st, a : a + 1],
+                    in1=baseT[:, st, :], op0=ALU.add, op1=ALU.add,
+                )
+            if a % 2 == 0:
+                stage = stream.tile([P, NB, 2, S_OUT], F32, name="stage", tag="stage", bufs=3)
+            tag = "pt" if a % 2 == 0 else "pm"
+            psos = []
+            for hb in range(2):
+                pso = psum.tile([P, 2, S_OUT], F32, name="pso", tag=tag, bufs=2)
+                for bl in range(2):
+                    bt = 2 * hb + bl
+                    for st in range(2):
+                        nc.tensor.transpose(
+                            pso[:, bl, P * st : P * (st + 1)],
+                            advT[:, st, P * bt : P * (bt + 1)],
+                            ident_f[:],
+                        )
+                psos.append(pso)
+            m2(a + 2)
+            for hb in range(2):
+                nc.scalar.copy(out=stage[:, 2 * hb : 2 * hb + 2, a % 2, :], in_=psos[hb][:])
+                if a >= ACTIONS - 2:
+                    nc.sync.dma_start(
+                        out=out[2 * P * hb : 2 * P * (hb + 1), a, :].rearrange("(b n) s -> n b s", n=P),
+                        in_=stage[:, 2 * hb : 2 * hb + 2, a % 2, :],
+                    )
+            if a % 2 == 1 and a < ACTIONS - 2:
+                nc.sync.dma_start(
+                    out=out[:, a - 1 : a + 1, :].rearrange("(b n) a s -> n b a s", n=P), in_=stage[:]
+                )

@@ -22,6 +22,7 @@ LAST = ACTIONS
 BANK_DT = BF16
 MS = 16
 FAST_COPY = True
+STRAIGHT = [4, 9, 14, 15]
 
 FLOPS = 2 * (ACTIONS + 1) * BATCH * F * (F + S_OUT)
 
@@ -49,6 +50,8 @@ def tile_psicritic_pa_kernel(tc, h1, W2, b2, W3, b3, g1, V2, c2, V3, c3, out):
         h2s = keep.tile([P, LAST + 1, BATCH], U8, name="h2s", align_bytes=64)
         stT = keep.tile([P, 2, BATCH], F32, name="stT")
         baseT = keep.tile([P, 2, BATCH], F32, name="baseT")
+        baseN = keep.tile([P, NB, S_OUT], F32, name="baseN")
+        b3b = keep.tile([P, len(STRAIGHT), S_OUT], BF16, name="b3b")
 
         t = {}
 
@@ -58,15 +61,15 @@ def tile_psicritic_pa_kernel(tc, h1, W2, b2, W3, b3, g1, V2, c2, V3, c3, out):
         def load(i):
             if not ok(i):
                 return
-            x = stream.tile([P, NB, F], BF16, name="x", tag="x", bufs=5)
+            x = stream.tile([P, NB, F], BF16, name="x", tag="x", bufs=4)
             srcx = g1 if i == 0 else h1[:, i - 1, :]
             nc.sync.dma_start(out=x[:], in_=srcx.rearrange("(b n) k -> n b k", n=P))
             t["x", i] = x
-            raw2 = stream.tile([P, 4, F], BF16, name="raw2", tag="raw2", bufs=5)
+            raw2 = stream.tile([P, 4, F], BF16, name="raw2", tag="raw2", bufs=4)
             src2 = V2 if i == 0 else W2[i - 1, :, :]
             nc.sync.dma_start(out=raw2[:], in_=src2.rearrange("(p j) c -> p j c", j=4))
             t["raw2", i] = raw2
-            raw3 = stream.tile([P, 4, S_OUT], BF16, name="raw3", tag="raw3", bufs=5)
+            raw3 = stream.tile([P, 4, S_OUT], BF16, name="raw3", tag="raw3", bufs=4)
             src3 = V3 if i == 0 else W3[i - 1, :, :]
             nc.sync.dma_start(out=raw3[:], in_=src3.rearrange("(p j) s -> p j s", j=4))
             t["raw3", i] = raw3
@@ -74,10 +77,10 @@ def tile_psicritic_pa_kernel(tc, h1, W2, b2, W3, b3, g1, V2, c2, V3, c3, out):
         def wi2s(i):
             if not ok(i):
                 return
-            w2g = stream.tile([P, 4 * F], BF16, name="w2g", tag="w2g", bufs=3, align_bytes=64)
-            t["w2g", i] = w2g
+            pair = stream.tile([P, 4 * F + 4 * BATCH], BF16, name="pair", tag="pair", bufs=2, align_bytes=64)
+            t["pair", i] = pair
             nc.scalar.copy(
-                out=w2g[:].rearrange("p (t m j) -> p t m j", t=4, j=4)[:, :, P - MS : P, :],
+                out=pair[:, 0 : 4 * F].rearrange("p (t m j) -> p t m j", t=4, j=4)[:, :, P - MS : P, :],
                 in_=t["raw2", i][:].rearrange("p j (m t) -> p t m j", t=4)[:, :, P - MS : P, :],
             )
 
@@ -85,18 +88,18 @@ def tile_psicritic_pa_kernel(tc, h1, W2, b2, W3, b3, g1, V2, c2, V3, c3, out):
             if not ok(i):
                 return
             nc.vector.tensor_copy(
-                out=t["w2g", i][:].rearrange("p (t m j) -> p t m j", t=4, j=4)[:, :, 0 : P - MS, :],
+                out=t["pair", i][:, 0 : 4 * F].rearrange("p (t m j) -> p t m j", t=4, j=4)[:, :, 0 : P - MS, :],
                 in_=t["raw2", i][:].rearrange("p j (m t) -> p t m j", t=4)[:, :, 0 : P - MS, :],
             )
 
-        def q_w2(i):
+        def q_pair(i):
             if not ok(i):
                 return
-            w2c = stream.tile([P, F], U32, name="w2c", tag="w2c", bufs=3, align_bytes=64)
-            w2sc = stream.tile([P, F], U8, name="w2sc", tag="w2sc", bufs=3, align_bytes=64)
-            nc.vector.quantize_mx(out=w2c[:].bitcast(FP8X4), scales=w2sc[:], in_=t["w2g", i][:])
-            t["w2c", i] = w2c
-            t["w2sc", i] = w2sc
+            pc = stream.tile([P, F + BATCH], U32, name="pc", tag="pc", bufs=3, align_bytes=64)
+            psc = stream.tile([P, F + BATCH], U8, name="psc", tag="psc", bufs=3, align_bytes=64)
+            nc.vector.quantize_mx(out=pc[:].bitcast(FP8X4), scales=psc[:], in_=t["pair", i][:])
+            t["pc", i] = pc
+            t["psc", i] = psc
 
         def wa3(i):
             if not ok(i):
@@ -139,24 +142,12 @@ def tile_psicritic_pa_kernel(tc, h1, W2, b2, W3, b3, g1, V2, c2, V3, c3, out):
         def htc(i, hb):
             if not ok(i):
                 return
-            if hb == 0:
-                xg = stream.tile([P, 4 * BATCH], BF16, name="xg", tag="xg", bufs=2, align_bytes=64)
-                t["xg", i] = xg
             nc.scalar.copy(
-                out=t["xg", i][:, 1024 * hb : 1024 * (hb + 1)]
+                out=t["pair", i][:, 4 * F + 1024 * hb : 4 * F + 1024 * (hb + 1)]
                 .bitcast(F32)
                 .rearrange("p (b n u) -> p b n u", b=2, u=2),
                 in_=t["pt", i, hb][:].rearrange("p b u n -> p b n u"),
             )
-
-        def q_x(i):
-            if not ok(i):
-                return
-            xc = stream.tile([P, BATCH], U32, name="xc", tag="xc", bufs=2, align_bytes=64)
-            xsc = stream.tile([P, BATCH], U8, name="xsc", tag="xsc", bufs=2, align_bytes=64)
-            nc.vector.quantize_mx(out=xc[:].bitcast(FP8X4), scales=xsc[:], in_=t["xg", i][:])
-            t["xc", i] = xc
-            t["xsc", i] = xsc
 
         def m1(i, tt):
             if not ok(i):
@@ -165,10 +156,10 @@ def tile_psicritic_pa_kernel(tc, h1, W2, b2, W3, b3, g1, V2, c2, V3, c3, out):
             cols = slice(P * tt, P * (tt + 1))
             nc.tensor.matmul_mx(
                 out=ps1[:],
-                lhsT=t["w2c", i][:, cols].bitcast(FP8X4),
-                lhsT_scale=t["w2sc", i][:, cols],
-                rhs=t["xc", i][:].bitcast(FP8X4),
-                rhs_scale=t["xsc", i][:],
+                lhsT=t["pc", i][:, cols].bitcast(FP8X4),
+                lhsT_scale=t["psc", i][:, cols],
+                rhs=t["pc", i][:, F : F + BATCH].bitcast(FP8X4),
+                rhs_scale=t["psc", i][:, F : F + BATCH],
                 start=True,
                 stop=True,
             )
@@ -266,19 +257,23 @@ def tile_psicritic_pa_kernel(tc, h1, W2, b2, W3, b3, g1, V2, c2, V3, c3, out):
 
         for i in range(-3, LAST + 3):
             load(i + 5)
+            if i == 12:
+                for g in range(len(STRAIGHT)):
+                    nc.sync.dma_start(out=b3b[:, g, :], in_=b3[STRAIGHT[g], :].partition_broadcast(P))
             s1b(i - 1)
-            q_x(i + 1)
-            q_h2(i - 1)
-            s1a(i, 0)
-            m1(i, 3)
             htc(i + 2, 0)
             tr_x(i + 3, 0)
+            htc(i + 2, 1)
+            tr_x(i + 3, 1)
+            wi2v(i + 2)
+            q_h2(i - 1)
+            q_w3(i + 1)
+            s1a(i, 0)
+            m1(i, 3)
             s1a(i, 1)
             m1(i + 1, 0)
             s1a(i, 2)
             m1(i + 1, 1)
-            htc(i + 2, 1)
-            tr_x(i + 3, 1)
             s1a(i, 3)
             m1(i + 1, 2)
             mm_mean(i - 1, 0)
@@ -288,9 +283,7 @@ def tile_psicritic_pa_kernel(tc, h1, W2, b2, W3, b3, g1, V2, c2, V3, c3, out):
             wi2s(i + 3)
             if i == -2:
                 bias_prep_pe()
-            wi2v(i + 2)
-            q_w3(i + 1)
-            q_w2(i + 2)
+            q_pair(i + 2)
             if i == -2:
                 bias_prep_v()
             if i == 1:
@@ -299,55 +292,95 @@ def tile_psicritic_pa_kernel(tc, h1, W2, b2, W3, b3, g1, V2, c2, V3, c3, out):
                         out=stT[:, st, :], in0=t["pm", st][:], scalar1=kb[:, st : st + 1]
                     )
 
+        def straight(a):
+            return a in STRAIGHT
+
         def m2(a):
             if a >= ACTIONS:
                 return
-            for st in range(2):
-                if a % 2 == 1 and st == 1:
-                    ps2 = psum.tile([P, BATCH], F32, name="ps2", tag="pw", bufs=1)
+            for h in range(2):
+                shape = [P, 2, S_OUT] if straight(a) else [P, BATCH]
+                if a % 2 == 1 and h == 1:
+                    ps2 = psum.tile(shape, F32, name="ps2", tag="pw", bufs=1)
                 else:
-                    ps2 = psum.tile([P, BATCH], F32, name="ps2", tag="ps1", bufs=3)
-                mm2(ps2[:], a + 1, st, True, True)
-                t["ps2", a, st] = ps2
+                    ps2 = psum.tile(shape, F32, name="ps2", tag="ps1", bufs=3)
+                t["ps2", a, h] = ps2
+                if straight(a):
+                    for bl in range(2):
+                        rows = slice(P * (2 * h + bl), P * (2 * h + bl + 1))
+                        nc.tensor.matmul_mx(
+                            out=ps2[:, bl, :],
+                            lhsT=h2q[:, a + 1, rows].bitcast(FP8X4),
+                            lhsT_scale=h2s[:, a + 1, rows],
+                            rhs=w3q[:, a + 1, :].bitcast(FP8X4),
+                            rhs_scale=w3s[:, a + 1, :],
+                            start=True,
+                            stop=True,
+                        )
+                else:
+                    mm2(ps2[:], a + 1, h, True, True)
 
-        for st in range(2):
-            nc.vector.scalar_tensor_tensor(
-                out=baseT[:, st, :], in0=t["pm", st][:], scalar=-1.0 / ACTIONS, in1=stT[:, st, :],
-                op0=ALU.mult, op1=ALU.add,
-            )
-        m2(0)
-        m2(1)
-        for a in range(ACTIONS):
-            advT = stream.tile([P, 2, BATCH], F32, name="advT", tag="advT", bufs=3)
-            for st in range(2):
-                nc.vector.scalar_tensor_tensor(
-                    out=advT[:, st, :], in0=t["ps2", a, st][:], scalar=b3T[:, st, a : a + 1],
-                    in1=baseT[:, st, :], op0=ALU.add, op1=ALU.add,
-                )
-            if a % 2 == 0:
-                stage = stream.tile([P, NB, 2, S_OUT], F32, name="stage", tag="stage", bufs=3)
-            tag = "pt" if a % 2 == 0 else "pm"
-            psos = []
+        def turn(src, tag):
+            tiles = []
             for hb in range(2):
                 pso = psum.tile([P, 2, S_OUT], F32, name="pso", tag=tag, bufs=2)
                 for bl in range(2):
                     bt = 2 * hb + bl
                     for st in range(2):
                         nc.tensor.transpose(
-                            pso[:, bl, P * st : P * (st + 1)],
-                            advT[:, st, P * bt : P * (bt + 1)],
-                            ident_f[:],
+                            pso[:, bl, P * st : P * (st + 1)], src[:, st, P * bt : P * (bt + 1)], ident_f[:]
                         )
-                psos.append(pso)
-            m2(a + 2)
-            for hb in range(2):
-                nc.scalar.copy(out=stage[:, 2 * hb : 2 * hb + 2, a % 2, :], in_=psos[hb][:])
-                if a >= ACTIONS - 2:
+                tiles.append(pso)
+            return tiles
+
+        m2(0)
+        m2(1)
+        for st in range(2):
+            nc.vector.scalar_tensor_tensor(
+                out=baseT[:, st, :], in0=t["pm", st][:], scalar=-1.0 / ACTIONS, in1=stT[:, st, :],
+                op0=ALU.mult, op1=ALU.add,
+            )
+        pbn = turn(baseT, "pt")
+        for hb in range(2):
+            nc.scalar.copy(out=baseN[:, 2 * hb : 2 * hb + 2, :], in_=pbn[hb][:])
+        for g in range(len(STRAIGHT)):
+            t2 = stream.tile([P, NB, S_OUT], F32, name="t2", tag="t2", bufs=2)
+            nc.gpsimd.tensor_tensor(
+                out=t2[:], in0=baseN[:], in1=b3b[:, g : g + 1, :].to_broadcast([P, NB, S_OUT]), op=ALU.add
+            )
+            t["t2", STRAIGHT[g]] = t2
+
+        turned = 0
+        for a in range(ACTIONS):
+            if a % 2 == 0:
+                stage = stream.tile([P, NB, 2, S_OUT], F32, name="stage", tag="stage", bufs=3)
+            late = a >= ACTIONS - 2
+            if straight(a):
+                for hb in range(2):
+                    nc.vector.tensor_tensor(
+                        out=stage[:, 2 * hb : 2 * hb + 2, a % 2, :], in0=t["ps2", a, hb][:],
+                        in1=t["t2", a][:, 2 * hb : 2 * hb + 2, :], op=ALU.add,
+                    )
+                m2(a + 2)
+            else:
+                advT = stream.tile([P, 2, BATCH], F32, name="advT", tag="advT", bufs=3)
+                for st in range(2):
+                    nc.vector.scalar_tensor_tensor(
+                        out=advT[:, st, :], in0=t["ps2", a, st][:], scalar=b3T[:, st, a : a + 1],
+                        in1=baseT[:, st, :], op0=ALU.add, op1=ALU.add,
+                    )
+                m2(a + 2)
+                psos = turn(advT, "pm" if turned % 2 == 0 else "pt")
+                turned += 1
+                for hb in range(2):
+                    nc.scalar.copy(out=stage[:, 2 * hb : 2 * hb + 2, a % 2, :], in_=psos[hb][:])
+            if late:
+                for hb in range(2):
                     nc.sync.dma_start(
                         out=out[2 * P * hb : 2 * P * (hb + 1), a, :].rearrange("(b n) s -> n b s", n=P),
                         in_=stage[:, 2 * hb : 2 * hb + 2, a % 2, :],
                     )
-            if a % 2 == 1 and a < ACTIONS - 2:
+            elif a % 2 == 1:
                 nc.sync.dma_start(
                     out=out[:, a - 1 : a + 1, :].rearrange("(b n) a s -> n b a s", n=P), in_=stage[:]
                 )

@@ -353,7 +353,10 @@ def tile_psicritic_pa_kernel(tc, h1, W2, b2, W3, b3, g1, V2, c2, V3, c3, out):
         turned = 0
         for a in range(ACTIONS):
             if a % 2 == 0:
-                stage = stream.tile([P, NB, 2, S_OUT], F32, name="stage", tag="stage", bufs=3)
+                if (a // 2) % 5 < 3:
+                    stage = stream.tile([P, NB, 2, S_OUT], F32, name="stage", tag="stage", bufs=3)
+                else:
+                    stage = stream.tile([P, NB, 2, S_OUT], F32, name="stage", tag="pair", bufs=2, align_bytes=64)
             late = a >= ACTIONS - 2
             if straight(a):
                 for hb in range(2):
@@ -380,7 +383,14 @@ def tile_psicritic_pa_kernel(tc, h1, W2, b2, W3, b3, g1, V2, c2, V3, c3, out):
                         out=out[2 * P * hb : 2 * P * (hb + 1), a, :].rearrange("(b n) s -> n b s", n=P),
                         in_=stage[:, 2 * hb : 2 * hb + 2, a % 2, :],
                     )
+            elif a == ACTIONS - 3:
+                held = stage
             elif a % 2 == 1:
                 nc.sync.dma_start(
                     out=out[:, a - 1 : a + 1, :].rearrange("(b n) a s -> n b a s", n=P), in_=stage[:]
                 )
+        for hb in range(2):
+            nc.sync.dma_start(
+                out=out[2 * P * hb : 2 * P * (hb + 1), ACTIONS - 4 : ACTIONS - 2, :].rearrange("(b n) a s -> n b a s", n=P),
+                in_=held[:, 2 * hb : 2 * hb + 2, :, :],
+            )

@@ -20,7 +20,7 @@ F = 512
 NB = BATCH // P
 LAST = ACTIONS
 BANK_DT = BF16
-MS = 16
+MS = 32
 FAST_COPY = True
 STRAIGHT = [4, 9, 14, 15]
 

@@ -80,16 +80,16 @@ def tile_psicritic_pa_kernel(tc, h1, W2, b2, W3, b3, g1, V2, c2, V3, c3, out):
             pair = stream.tile([P, 4 * F + 4 * BATCH], BF16, name="pair", tag="pair", bufs=2, align_bytes=64)
             t["pair", i] = pair
             nc.scalar.copy(
-                out=pair[:, 0 : 4 * F].rearrange("p (t m j) -> p t m j", t=4, j=4)[:, :, P - MS : P, :],
-                in_=t["raw2", i][:].rearrange("p j (m t) -> p t m j", t=4)[:, :, P - MS : P, :],
+                out=pair[:, 0 : 4 * F].rearrange("p (t m j) -> p m j t", t=4, j=4)[:, P - MS : P, :, :],
+                in_=t["raw2", i][:].rearrange("p j (m t) -> p m j t", t=4)[:, P - MS : P, :, :],
             )
 
         def wi2v(i):
             if not ok(i):
                 return
             nc.vector.tensor_copy(
-                out=t["pair", i][:, 0 : 4 * F].rearrange("p (t m j) -> p t m j", t=4, j=4)[:, :, 0 : P - MS, :],
-                in_=t["raw2", i][:].rearrange("p j (m t) -> p t m j", t=4)[:, :, 0 : P - MS, :],
+                out=t["pair", i][:, 0 : 4 * F].rearrange("p (t m j) -> p m j t", t=4, j=4)[:, 0 : P - MS, :, :],
+                in_=t["raw2", i][:].rearrange("p j (m t) -> p m j t", t=4)[:, 0 : P - MS, :, :],
             )
 
         def q_pair(i):

@@ -80,16 +80,16 @@ def tile_psicritic_pa_kernel(tc, h1, W2, b2, W3, b3, g1, V2, c2, V3, c3, out):
             pair = stream.tile([P, 4 * F + 4 * BATCH], BF16, name="pair", tag="pair", bufs=2, align_bytes=64)
             t["pair", i] = pair
             nc.scalar.copy(
-                out=pair[:, 0 : 4 * F].rearrange("p (t m j) -> p m j t", t=4, j=4)[:, P - MS : P, :, :],
-                in_=t["raw2", i][:].rearrange("p j (m t) -> p m j t", t=4)[:, P - MS : P, :, :],
+                out=pair[:, 0 : 4 * F].rearrange("p (t c e j) -> p c j t e", t=4, e=2, j=4)[:, (P - MS) // 2 : P // 2],
+                in_=t["raw2", i][:].rearrange("p j (c e t) -> p c j t e", e=2, t=4)[:, (P - MS) // 2 : P // 2],
             )
 
         def wi2v(i):
             if not ok(i):
                 return
             nc.vector.tensor_copy(
-                out=t["pair", i][:, 0 : 4 * F].rearrange("p (t m j) -> p m j t", t=4, j=4)[:, 0 : P - MS, :, :],
-                in_=t["raw2", i][:].rearrange("p j (m t) -> p m j t", t=4)[:, 0 : P - MS, :, :],
+                out=t["pair", i][:, 0 : 4 * F].rearrange("p (t c e j) -> p c j t e", t=4, e=2, j=4)[:, 0 : (P - MS) // 2],
+                in_=t["raw2", i][:].rearrange("p j (c e t) -> p c j t e", e=2, t=4)[:, 0 : (P - MS) // 2],
             )
 
         def q_pair(i):
@@ -186,8 +186,8 @@ def tile_psicritic_pa_kernel(tc, h1, W2, b2, W3, b3, g1, V2, c2, V3, c3, out):
             h2g = stream.tile([P, 4 * BATCH], BF16, name="h2g", tag="h2g", bufs=2, align_bytes=64)
             if FAST_COPY:
                 nc.vector.tensor_copy(
-                    out=h2g[:].rearrange("p (c i j) -> p c j i", i=4, j=4),
-                    in_=t["h2c", i][:].rearrange("p j (c i) -> p c j i", i=4),
+                    out=h2g[:].rearrange("p (c i j) -> p c j i", i=8, j=4),
+                    in_=t["h2c", i][:].rearrange("p j (c i) -> p c j i", i=8),
                 )
             else:
                 nc.vector.tensor_copy(

@@ -20,7 +20,7 @@ F = 512
 NB = BATCH // P
 LAST = ACTIONS
 BANK_DT = BF16
-MS = 32
+MS = 24
 FAST_COPY = True
 STRAIGHT = [4, 9, 14, 15]
 

@@ -357,7 +357,7 @@ def tile_psicritic_pa_kernel(tc, h1, W2, b2, W3, b3, g1, V2, c2, V3, c3, out):
                     stage = stream.tile([P, NB, 2, S_OUT], F32, name="stage", tag="stage", bufs=3)
                 else:
                     stage = stream.tile([P, NB, 2, S_OUT], F32, name="stage", tag="pair", bufs=2, align_bytes=64)
-            late = a >= ACTIONS - 2
+            late = a >= ACTIONS - 2 or a < 2
             if straight(a):
                 for hb in range(2):
                     nc.vector.tensor_tensor(

@@ -152,10 +152,13 @@ def tile_psicritic_pa_kernel(tc, h1, W2, b2, W3, b3, g1, V2, c2, V3, c3, out):
         def m1(i, tt):
             if not ok(i):
                 return
-            ps1 = psum.tile([P, BATCH], BANK_DT, name="ps1", tag="ps1", bufs=3)
+            if tt % 2 == 0:
+                ps1 = psum.tile([P, 2, BATCH], BANK_DT, name="ps1", tag="ps1", bufs=3)
+                t["ps1", i, tt // 2] = ps1
+            ps1 = t["ps1", i, tt // 2]
             cols = slice(P * tt, P * (tt + 1))
             nc.tensor.matmul_mx(
-                out=ps1[:],
+                out=ps1[:, tt % 2, :],
                 lhsT=t["pc", i][:, cols].bitcast(FP8X4),
                 lhsT_scale=t["psc", i][:, cols],
                 rhs=t["pc", i][:, F : F + BATCH].bitcast(FP8X4),
@@ -163,7 +166,6 @@ def tile_psicritic_pa_kernel(tc, h1, W2, b2, W3, b3, g1, V2, c2, V3, c3, out):
                 start=True,
                 stop=True,
             )
-            t["ps1", i, tt] = ps1
 
         def s1a(i, tt):
             if not ok(i):
@@ -174,7 +176,7 @@ def tile_psicritic_pa_kernel(tc, h1, W2, b2, W3, b3, g1, V2, c2, V3, c3, out):
                 t["h2c", i] = h2c
             nc.scalar.activation(
                 out=t["h2c", i][:, tt, :],
-                in_=t["ps1", i, tt][:],
+                in_=t["ps1", i, tt // 2][:, tt % 2, :],
                 func=ACT.Relu,
                 bias=b2T[:, tt, row : row + 1],
                 scale=1.0,
@@ -269,19 +271,19 @@ def tile_psicritic_pa_kernel(tc, h1, W2, b2, W3, b3, g1, V2, c2, V3, c3, out):
             q_h2(i - 1)
             q_w3(i + 1)
             s1a(i, 0)
-            m1(i, 3)
-            s1a(i, 1)
             m1(i + 1, 0)
-            s1a(i, 2)
+            s1a(i, 1)
             m1(i + 1, 1)
-            s1a(i, 3)
+            s1a(i, 2)
             m1(i + 1, 2)
+            s1a(i, 3)
+            m1(i + 1, 3)
             mm_mean(i - 1, 0)
             mm_mean(i - 1, 1)
             w3copy(i + 2)
             wa3(i + 3)
             wi2s(i + 3)
-            if i == -2:
+            if i == -3:
                 bias_prep_pe()
             q_pair(i + 2)
             if i == -2:

@@ -62,15 +62,15 @@ def tile_psicritic_pa_kernel(tc, h1, W2, b2, W3, b3, g1, V2, c2, V3, c3, out):
             if not ok(i):
                 return
             x = stream.tile([P, NB, F], BF16, name="x", tag="x", bufs=4)
-            srcx = g1 if i == 0 else h1[:, i - 1, :]
+            srcx = g1 if i == LAST else h1[:, i, :]
             nc.sync.dma_start(out=x[:], in_=srcx.rearrange("(b n) k -> n b k", n=P))
             t["x", i] = x
             raw2 = stream.tile([P, 4, F], BF16, name="raw2", tag="raw2", bufs=4)
-            src2 = V2 if i == 0 else W2[i - 1, :, :]
+            src2 = V2 if i == LAST else W2[i, :, :]
             nc.sync.dma_start(out=raw2[:], in_=src2.rearrange("(p j) c -> p j c", j=4))
             t["raw2", i] = raw2
             raw3 = stream.tile([P, 4, S_OUT], BF16, name="raw3", tag="raw3", bufs=4)
-            src3 = V3 if i == 0 else W3[i - 1, :, :]
+            src3 = V3 if i == LAST else W3[i, :, :]
             nc.sync.dma_start(out=raw3[:], in_=src3.rearrange("(p j) s -> p j s", j=4))
             t["raw3", i] = raw3
 
@@ -170,7 +170,7 @@ def tile_psicritic_pa_kernel(tc, h1, W2, b2, W3, b3, g1, V2, c2, V3, c3, out):
         def s1a(i, tt):
             if not ok(i):
                 return
-            row = LAST if i == 0 else i - 1
+            row = i
             if tt == 0:
                 h2c = stream.tile([P, 4, BATCH], BF16, name="h2c", tag="h2c", bufs=2)
                 t["h2c", i] = h2c
@@ -220,10 +220,10 @@ def tile_psicritic_pa_kernel(tc, h1, W2, b2, W3, b3, g1, V2, c2, V3, c3, out):
         def mm_mean(i, st):
             if not ok(i):
                 return
-            if i <= 1:
+            if i == 0 or i == LAST:
                 pm = psum.tile([P, BATCH], F32, name="pm", tag="pm", bufs=2)
                 t["pm", st] = pm
-            mm2(t["pm", st][:], i, st, i <= 1, i == 0 or i == LAST)
+            mm2(t["pm", st][:], i, st, i == 0 or i == LAST, i >= LAST - 1)
 
         def bias_prep_pe():
             pb2 = psum.tile([P, 4, P], BF16, name="pb2", tag="pm", bufs=2)
@@ -280,6 +280,11 @@ def tile_psicritic_pa_kernel(tc, h1, W2, b2, W3, b3, g1, V2, c2, V3, c3, out):
             m1(i + 1, 3)
             mm_mean(i - 1, 0)
             mm_mean(i - 1, 1)
+            if i == LAST:
+                for st in range(2):
+                    nc.scalar.activation(
+                        out=stT[:, st, :], in_=t["pm", st][:], func=ACT.Identity, bias=kb[:, st : st + 1], scale=-1.0 / ACTIONS
+                    )
             w3copy(i + 2)
             wa3(i + 3)
             wi2s(i + 3)
@@ -288,11 +293,6 @@ def tile_psicritic_pa_kernel(tc, h1, W2, b2, W3, b3, g1, V2, c2, V3, c3, out):
             q_pair(i + 2)
             if i == -2:
                 bias_prep_v()
-            if i == 1:
-                for st in range(2):
-                    nc.vector.tensor_scalar_add(
-                        out=stT[:, st, :], in0=t["pm", st][:], scalar1=kb[:, st : st + 1]
-                    )
 
         def straight(a):
             return a in STRAIGHT
@@ -312,15 +312,15 @@ def tile_psicritic_pa_kernel(tc, h1, W2, b2, W3, b3, g1, V2, c2, V3, c3, out):
                         rows = slice(P * (2 * h + bl), P * (2 * h + bl + 1))
                         nc.tensor.matmul_mx(
                             out=ps2[:, bl, :],
-                            lhsT=h2q[:, a + 1, rows].bitcast(FP8X4),
-                            lhsT_scale=h2s[:, a + 1, rows],
-                            rhs=w3q[:, a + 1, :].bitcast(FP8X4),
-                            rhs_scale=w3s[:, a + 1, :],
+                            lhsT=h2q[:, a, rows].bitcast(FP8X4),
+                            lhsT_scale=h2s[:, a, rows],
+                            rhs=w3q[:, a, :].bitcast(FP8X4),
+                            rhs_scale=w3s[:, a, :],
                             start=True,
                             stop=True,
                         )
                 else:
-                    mm2(ps2[:], a + 1, h, True, True)
+                    mm2(ps2[:], a, h, True, True)
 
         def turn(src, tag):
             tiles = []
@@ -338,10 +338,7 @@ def tile_psicritic_pa_kernel(tc, h1, W2, b2, W3, b3, g1, V2, c2, V3, c3, out):
         m2(0)
         m2(1)
         for st in range(2):
-            nc.vector.scalar_tensor_tensor(
-                out=baseT[:, st, :], in0=t["pm", st][:], scalar=-1.0 / ACTIONS, in1=stT[:, st, :],
-                op0=ALU.mult, op1=ALU.add,
-            )
+            nc.vector.tensor_tensor(out=baseT[:, st, :], in0=t["pm", st][:], in1=stT[:, st, :], op=ALU.add)
         pbn = turn(baseT, "pt")
         for hb in range(2):
             nc.scalar.copy(out=baseN[:, 2 * hb : 2 * hb + 2, :], in_=pbn[hb][:])
@@ -388,9 +385,11 @@ def tile_psicritic_pa_kernel(tc, h1, W2, b2, W3, b3, g1, V2, c2, V3, c3, out):
             elif a == ACTIONS - 3:
                 held = stage
             elif a % 2 == 1:
-                nc.sync.dma_start(
-                    out=out[:, a - 1 : a + 1, :].rearrange("(b n) a s -> n b a s", n=P), in_=stage[:]
-                )
+                for hb in range(2):
+                    nc.sync.dma_start(
+                        out=out[2 * P * hb : 2 * P * (hb + 1), a - 1 : a + 1, :].rearrange("(b n) a s -> n b a s", n=P),
+                        in_=stage[:, 2 * hb : 2 * hb + 2, :, :],
+                    )
         for hb in range(2):
             nc.sync.dma_start(
                 out=out[2 * P * hb : 2 * P * (hb + 1), ACTIONS - 4 : ACTIONS - 2, :].rearrange("(b n) a s -> n b a s", n=P),

@@ -20,7 +20,7 @@ F = 512
 NB = BATCH // P
 LAST = ACTIONS
 BANK_DT = BF16
-MS = 24
+MS = 20
 FAST_COPY = True
 STRAIGHT = [4, 9, 14, 15]
 

@@ -21,7 +21,8 @@ NB = BATCH // P
 LAST = ACTIONS
 BANK_DT = BF16
 MS = 20
-FAST_COPY = True
+HALF = BATCH // 2
+HALVES = [slice(0, HALF), slice(HALF, BATCH)]
 STRAIGHT = [4, 9, 14, 15]
 
 FLOPS = 2 * (ACTIONS + 1) * BATCH * F * (F + S_OUT)
@@ -167,42 +168,37 @@ def tile_psicritic_pa_kernel(tc, h1, W2, b2, W3, b3, g1, V2, c2, V3, c3, out):
                 stop=True,
             )
 
-        def s1a(i, tt):
+        def s1a(i, tt, cols=slice(0, BATCH)):
             if not ok(i):
                 return
             row = i
-            if tt == 0:
+            if tt == 0 and cols.start == 0:
                 h2c = stream.tile([P, 4, BATCH], BF16, name="h2c", tag="h2c", bufs=2)
                 t["h2c", i] = h2c
             nc.scalar.activation(
-                out=t["h2c", i][:, tt, :],
-                in_=t["ps1", i, tt // 2][:, tt % 2, :],
+                out=t["h2c", i][:, tt, cols],
+                in_=t["ps1", i, tt // 2][:, tt % 2, cols],
                 func=ACT.Relu,
                 bias=b2T[:, tt, row : row + 1],
                 scale=1.0,
             )
 
-        def s1b(i):
+        def s1b(i, cols=slice(0, BATCH)):
             if not ok(i):
                 return
-            h2g = stream.tile([P, 4 * BATCH], BF16, name="h2g", tag="h2g", bufs=2, align_bytes=64)
-            if FAST_COPY:
-                nc.vector.tensor_copy(
-                    out=h2g[:].rearrange("p (c i j) -> p c j i", i=8, j=4),
-                    in_=t["h2c", i][:].rearrange("p j (c i) -> p c j i", i=8),
-                )
-            else:
-                nc.vector.tensor_copy(
-                    out=h2g[:].rearrange("p (n j) -> p n j", j=4),
-                    in_=t["h2c", i][:].rearrange("p j n -> p n j"),
-                )
-            t["h2g", i] = h2g
+            if cols.start == 0:
+                h2g = stream.tile([P, 4 * BATCH], BF16, name="h2g", tag="h2g", bufs=2, align_bytes=64)
+                t["h2g", i] = h2g
+            nc.vector.tensor_copy(
+                out=t["h2g", i][:, 4 * cols.start : 4 * cols.stop].rearrange("p (c i j) -> p c j i", i=8, j=4),
+                in_=t["h2c", i][:, :, cols].rearrange("p j (c i) -> p c j i", i=8),
+            )
 
-        def q_h2(i):
+        def q_h2(i, cols=slice(0, BATCH)):
             if not ok(i):
                 return
             nc.vector.quantize_mx(
-                out=h2q[:, i, :].bitcast(FP8X4), scales=h2s[:, i, :], in_=t["h2g", i][:]
+                out=h2q[:, i, cols].bitcast(FP8X4), scales=h2s[:, i, cols], in_=t["h2g", i][:, 4 * cols.start : 4 * cols.stop]
             )
 
         def mm2(dst, i, st, start, stop):
@@ -220,10 +216,24 @@ def tile_psicritic_pa_kernel(tc, h1, W2, b2, W3, b3, g1, V2, c2, V3, c3, out):
         def mm_mean(i, st):
             if not ok(i):
                 return
-            if i == 0 or i == LAST:
+            if i == 0:
                 pm = psum.tile([P, BATCH], F32, name="pm", tag="pm", bufs=2)
                 t["pm", st] = pm
-            mm2(t["pm", st][:], i, st, i == 0 or i == LAST, i >= LAST - 1)
+            mm2(t["pm", st][:], i, st, i == 0, i == LAST - 1)
+
+        def mm_state(hf):
+            pst = psum.tile([P, 2, HALF], F32, name="pst", tag="pt", bufs=2)
+            for st in range(2):
+                nc.tensor.matmul_mx(
+                    out=pst[:, st, :],
+                    lhsT=w3q[:, LAST, P * st : P * (st + 1)].bitcast(FP8X4),
+                    lhsT_scale=w3s[:, LAST, P * st : P * (st + 1)],
+                    rhs=h2q[:, LAST, HALVES[hf]].bitcast(FP8X4),
+                    rhs_scale=h2s[:, LAST, HALVES[hf]],
+                    start=True,
+                    stop=True,
+                )
+            t["pst", hf] = pst
 
         def bias_prep_pe():
             pb2 = psum.tile([P, 4, P], BF16, name="pb2", tag="pm", bufs=2)
@@ -262,29 +272,42 @@ def tile_psicritic_pa_kernel(tc, h1, W2, b2, W3, b3, g1, V2, c2, V3, c3, out):
             if i == 12:
                 for g in range(len(STRAIGHT)):
                     nc.sync.dma_start(out=b3b[:, g, :], in_=b3[STRAIGHT[g], :].partition_broadcast(P))
-            s1b(i - 1)
+            if i - 1 < LAST:
+                s1b(i - 1)
             htc(i + 2, 0)
             tr_x(i + 3, 0)
             htc(i + 2, 1)
             tr_x(i + 3, 1)
             wi2v(i + 2)
-            q_h2(i - 1)
+            if i - 1 < LAST:
+                q_h2(i - 1)
             q_w3(i + 1)
-            s1a(i, 0)
-            m1(i + 1, 0)
-            s1a(i, 1)
-            m1(i + 1, 1)
-            s1a(i, 2)
-            m1(i + 1, 2)
-            s1a(i, 3)
-            m1(i + 1, 3)
-            mm_mean(i - 1, 0)
-            mm_mean(i - 1, 1)
+            if i < LAST:
+                s1a(i, 0)
+                m1(i + 1, 0)
+                s1a(i, 1)
+                m1(i + 1, 1)
+                s1a(i, 2)
+                m1(i + 1, 2)
+                s1a(i, 3)
+                m1(i + 1, 3)
+            if i - 1 < LAST:
+                mm_mean(i - 1, 0)
+                mm_mean(i - 1, 1)
             if i == LAST:
-                for st in range(2):
-                    nc.scalar.activation(
-                        out=stT[:, st, :], in_=t["pm", st][:], func=ACT.Identity, bias=kb[:, st : st + 1], scale=-1.0 / ACTIONS
-                    )
+                for hf in range(2):
+                    for tt in range(4):
+                        s1a(i, tt, HALVES[hf])
+                for hf in range(2):
+                    for st in range(2):
+                        nc.scalar.activation(
+                            out=stT[:, st, HALVES[hf]], in_=t["pm", st][:, HALVES[hf]], func=ACT.Identity,
+                            bias=kb[:, st : st + 1], scale=-1.0 / ACTIONS,
+                        )
+                for hf in range(2):
+                    s1b(i, HALVES[hf])
+                    q_h2(i, HALVES[hf])
+                    mm_state(hf)
             w3copy(i + 2)
             wa3(i + 3)
             wi2s(i + 3)
@@ -337,8 +360,10 @@ def tile_psicritic_pa_kernel(tc, h1, W2, b2, W3, b3, g1, V2, c2, V3, c3, out):
 
         m2(0)
         m2(1)
-        for st in range(2):
-            nc.vector.tensor_tensor(out=baseT[:, st, :], in0=t["pm", st][:], in1=stT[:, st, :], op=ALU.add)
+        for hf in range(2):
+            nc.vector.tensor_tensor(
+                out=baseT[:, :, HALVES[hf]], in0=t["pst", hf][:], in1=stT[:, :, HALVES[hf]], op=ALU.add
+            )
         pbn = turn(baseT, "pt")
         for hb in range(2):
             nc.scalar.copy(out=baseN[:, 2 * hb : 2 * hb + 2, :], in_=pbn[hb][:])

from contextlib import ExitStack

import concourse.mybir as mybir
from concourse.masks import make_identity

F32 = mybir.dt.float32
BF16 = mybir.dt.bfloat16
U32 = mybir.dt.uint32
U8 = mybir.dt.uint8
FP8X4 = mybir.dt.float8_e4m3fn_x4
ACT = mybir.ActivationFunctionType
ALU = mybir.AluOpType
AX = mybir.AxisListType

P = 128
BATCH = 512
ACTIONS = 16
S_OUT = 256
F = 512
NB = BATCH // P
LAST = ACTIONS
BANK_DT = BF16
MS = 20
HALF = BATCH // 2
HALVES = [slice(0, HALF), slice(HALF, BATCH)]
STRAIGHT = [4, 9, 14, 15]

FLOPS = 2 * (ACTIONS + 1) * BATCH * F * (F + S_OUT)


def tile_psicritic_pa_kernel(tc, h1, W2, b2, W3, b3, g1, V2, c2, V3, c3, out):
    nc = tc.nc
    with ExitStack() as ctx:
        keep = ctx.enter_context(tc.tile_pool(name="keep", bufs=1))
        stream = ctx.enter_context(tc.tile_pool(name="stream", bufs=2))
        psum = ctx.enter_context(tc.psum_pool(name="psum", bufs=2))
        ctx.enter_context(tc.manual_schedule())

        ident_f = keep.tile([P, P], F32, name="ident_f")
        ident_b = keep.tile([P, P], BF16, name="ident_b")
        brow2 = keep.tile([P, F], BF16, name="brow2")
        brow3 = keep.tile([P, S_OUT], BF16, name="brow3")
        b2T = keep.tile([P, 4, LAST + 1], F32, name="b2T")
        b3T = keep.tile([P, 2, LAST + 1], F32, name="b3T")
        bsum = keep.tile([P, 2], F32, name="bsum")
        kb = keep.tile([P, 2], F32, name="kb")
        warm = keep.tile([P, 1], F32, name="warm")
        w3q = keep.tile([P, LAST + 1, S_OUT], U32, name="w3q", align_bytes=64)
        w3s = keep.tile([P, LAST + 1, S_OUT], U8, name="w3s", align_bytes=64)
        h2q = keep.tile([P, LAST + 1, BATCH], U32, name="h2q", align_bytes=64)
        h2s = keep.tile([P, LAST + 1, BATCH], U8, name="h2s", align_bytes=64)
        stT = keep.tile([P, 2, BATCH], F32, name="stT")
        baseT = keep.tile([P, 2, BATCH], F32, name="baseT")
        baseN = keep.tile([P, NB, S_OUT], F32, name="baseN")
        b3b = keep.tile([P, len(STRAIGHT), S_OUT], BF16, name="b3b")

        t = {}

        def ok(i):
            return 0 <= i <= LAST

        def load(i):
            if not ok(i):
                return
            x = stream.tile([P, NB, F], BF16, name="x", tag="x", bufs=4)
            srcx = g1 if i == LAST else h1[:, i, :]
            nc.sync.dma_start(out=x[:], in_=srcx.rearrange("(b n) k -> n b k", n=P))
            t["x", i] = x
            raw2 = stream.tile([P, 4, F], BF16, name="raw2", tag="raw2", bufs=4)
            src2 = V2 if i == LAST else W2[i, :, :]
            nc.sync.dma_start(out=raw2[:], in_=src2.rearrange("(p j) c -> p j c", j=4))
            t["raw2", i] = raw2
            raw3 = stream.tile([P, 4, S_OUT], BF16, name="raw3", tag="raw3", bufs=4)
            src3 = V3 if i == LAST else W3[i, :, :]
            nc.sync.dma_start(out=raw3[:], in_=src3.rearrange("(p j) s -> p j s", j=4))
            t["raw3", i] = raw3

        def wi2s(i):
            if not ok(i):
                return
            pair = stream.tile([P, 4 * F + 4 * BATCH], BF16, name="pair", tag="pair", bufs=2, align_bytes=64)
            t["pair", i] = pair
            nc.scalar.copy(
                out=pair[:, 0 : 4 * F].rearrange("p (t c e j) -> p c j t e", t=4, e=2, j=4)[:, (P - MS) // 2 : P // 2],
                in_=t["raw2", i][:].rearrange("p j (c e t) -> p c j t e", e=2, t=4)[:, (P - MS) // 2 : P // 2],
            )

        def wi2v(i):
            if not ok(i):
                return
            nc.vector.tensor_copy(
                out=t["pair", i][:, 0 : 4 * F].rearrange("p (t c e j) -> p c j t e", t=4, e=2, j=4)[:, 0 : (P - MS) // 2],
                in_=t["raw2", i][:].rearrange("p j (c e t) -> p c j t e", e=2, t=4)[:, 0 : (P - MS) // 2],
            )

        def q_pair(i):
            if not ok(i):
                return
            pc = stream.tile([P, F + BATCH], U32, name="pc", tag="pc", bufs=3, align_bytes=64)
            psc = stream.tile([P, F + BATCH], U8, name="psc", tag="psc", bufs=3, align_bytes=64)
            nc.vector.quantize_mx(out=pc[:].bitcast(FP8X4), scales=psc[:], in_=t["pair", i][:])
            t["pc", i] = pc
            t["psc", i] = psc

        def wa3(i):
            if not ok(i):
                return
            pw = psum.tile([P, 4 * S_OUT], BF16, name="pw", tag="pw", bufs=1)
            for h in range(2):
                nc.tensor.matmul(
                    out=pw[:, 512 * h : 512 * (h + 1)].rearrange("p (s j) -> p s j", j=4),
                    lhsT=ident_b[:],
                    rhs=t["raw3", i][:, :, P * h : P * (h + 1)].rearrange("p j s -> p s j"),
                    start=True,
                    stop=True,
                )
            t["pw", i] = pw

        def w3copy(i):
            if not ok(i):
                return
            w3g = stream.tile([P, 4 * S_OUT], BF16, name="w3g", tag="w3g", bufs=2, align_bytes=64)
            nc.scalar.copy(out=w3g[:], in_=t["pw", i][:])
            t["w3g", i] = w3g

        def q_w3(i):
            if not ok(i):
                return
            nc.vector.quantize_mx(
                out=w3q[:, i, :].bitcast(FP8X4), scales=w3s[:, i, :], in_=t["w3g", i][:]
            )

        def tr_x(i, hb):
            if not ok(i):
                return
            pt = psum.tile([P, 2, 2, P], F32, name="pt", tag="pt", bufs=2)
            for bl in range(2):
                words = t["x", i][:, 2 * hb + bl, :].bitcast(F32)
                for u in range(2):
                    nc.tensor.transpose(pt[:, bl, u, :], words[:, u : F // 2 : 2], ident_f[:])
            t["pt", i, hb] = pt

        def htc(i, hb):
            if not ok(i):
                return
            nc.scalar.copy(
                out=t["pair", i][:, 4 * F + 1024 * hb : 4 * F + 1024 * (hb + 1)]
                .bitcast(F32)
                .rearrange("p (b n u) -> p b n u", b=2, u=2),
                in_=t["pt", i, hb][:].rearrange("p b u n -> p b n u"),
            )

        def m1(i, tt):
            if not ok(i):
                return
            if tt % 2 == 0:
                ps1 = psum.tile([P, 2, BATCH], BANK_DT, name="ps1", tag="ps1", bufs=3)
                t["ps1", i, tt // 2] = ps1
            ps1 = t["ps1", i, tt // 2]
            cols = slice(P * tt, P * (tt + 1))
            nc.tensor.matmul_mx(
                out=ps1[:, tt % 2, :],
                lhsT=t["pc", i][:, cols].bitcast(FP8X4),
                lhsT_scale=t["psc", i][:, cols],
                rhs=t["pc", i][:, F : F + BATCH].bitcast(FP8X4),
                rhs_scale=t["psc", i][:, F : F + BATCH],
                start=True,
                stop=True,
            )

        def s1a(i, tt, cols=slice(0, BATCH)):
            if not ok(i):
                return
            row = i
            if tt == 0 and cols.start == 0:
                h2c = stream.tile([P, 4, BATCH], BF16, name="h2c", tag="h2c", bufs=2)
                t["h2c", i] = h2c
            nc.scalar.activation(
                out=t["h2c", i][:, tt, cols],
                in_=t["ps1", i, tt // 2][:, tt % 2, cols],
                func=ACT.Relu,
                bias=b2T[:, tt, row : row + 1],
                scale=1.0,
            )

        def s1b(i, cols=slice(0, BATCH)):
            if not ok(i):
                return
            if cols.start == 0:
                h2g = stream.tile([P, 4 * BATCH], BF16, name="h2g", tag="h2g", bufs=2, align_bytes=64)
                t["h2g", i] = h2g
            nc.vector.tensor_copy(
                out=t["h2g", i][:, 4 * cols.start : 4 * cols.stop].rearrange("p (c i j) -> p c j i", i=8, j=4),
                in_=t["h2c", i][:, :, cols].rearrange("p j (c i) -> p c j i", i=8),
            )

        def q_h2(i, cols=slice(0, BATCH)):
            if not ok(i):
                return
            nc.vector.quantize_mx(
                out=h2q[:, i, cols].bitcast(FP8X4), scales=h2s[:, i, cols], in_=t["h2g", i][:, 4 * cols.start : 4 * cols.stop]
            )

        def mm2(dst, i, st, start, stop):
            cols = slice(P * st, P * (st + 1))
            nc.tensor.matmul_mx(
                out=dst,
                lhsT=w3q[:, i, cols].bitcast(FP8X4),
                lhsT_scale=w3s[:, i, cols],
                rhs=h2q[:, i, :].bitcast(FP8X4),
                rhs_scale=h2s[:, i, :],
                start=start,
                stop=stop,
            )

        def mm_mean(i, st):
            if not ok(i):
                return
            if i == 0:
                pm = psum.tile([P, BATCH], F32, name="pm", tag="pm", bufs=2)
                t["pm", st] = pm
            mm2(t["pm", st][:], i, st, i == 0, i == LAST - 1)

        def mm_state(hf):
            pst = psum.tile([P, 2, HALF], F32, name="pst", tag="pt", bufs=2)
            for st in range(2):
                nc.tensor.matmul_mx(
                    out=pst[:, st, :],
                    lhsT=w3q[:, LAST, P * st : P * (st + 1)].bitcast(FP8X4),
                    lhsT_scale=w3s[:, LAST, P * st : P * (st + 1)],
                    rhs=h2q[:, LAST, HALVES[hf]].bitcast(FP8X4),
                    rhs_scale=h2s[:, LAST, HALVES[hf]],
                    start=True,
                    stop=True,
                )
            t["pst", hf] = pst

        def bias_prep_pe():
            pb2 = psum.tile([P, 4, P], BF16, name="pb2", tag="pm", bufs=2)
            for tt in range(4):
                nc.tensor.transpose(pb2[:, tt, :], brow2[:, tt:F:4], ident_b[:])
            pb3 = psum.tile([P, 2, P], BF16, name="pb3", tag="pm", bufs=2)
            for st in range(2):
                nc.tensor.transpose(pb3[:, st, :], brow3[:, P * st : P * (st + 1)], ident_b[:])
            t["pb2"] = pb2
            t["pb3"] = pb3

        def bias_prep_v():
            nc.vector.tensor_copy(out=b2T[:], in_=t["pb2"][:, :, 0 : LAST + 1])
            nc.vector.tensor_copy(out=b3T[:], in_=t["pb3"][:, :, 0 : LAST + 1])
            nc.vector.tensor_reduce(out=bsum[:], in_=b3T[:, :, 0:ACTIONS], axis=AX.X, op=ALU.add)
            nc.vector.scalar_tensor_tensor(
                out=kb[:], in0=bsum[:], scalar=-1.0 / ACTIONS, in1=b3T[:, :, ACTIONS],
                op0=ALU.mult, op1=ALU.add,
            )

        nc.vector.memset(warm[:], 0.0)
        nc.vector.memset(brow2[:], 0.0)
        nc.vector.memset(brow3[:], 0.0)
        load(0)
        load(1)
        make_identity(nc, ident_f[:])
        make_identity(nc, ident_b[:])
        nc.scalar.dma_start(out=brow2[0:ACTIONS, :], in_=b2)
        nc.scalar.dma_start(out=brow2[ACTIONS : ACTIONS + 1, :], in_=c2.rearrange("(o f) -> o f", o=1))
        nc.scalar.dma_start(out=brow3[0:ACTIONS, :], in_=b3)
        nc.scalar.dma_start(out=brow3[ACTIONS : ACTIONS + 1, :], in_=c3.rearrange("(o f) -> o f", o=1))
        nc.scalar.activation(out=warm[:], in_=warm[:], func=ACT.Relu)

        for i in range(-3, LAST + 3):
            load(i + 5)
            if i == 12:
                for g in range(len(STRAIGHT)):
                    nc.sync.dma_start(out=b3b[:, g, :], in_=b3[STRAIGHT[g], :].partition_broadcast(P))
            if i - 1 < LAST:
                s1b(i - 1)
            htc(i + 2, 0)
            tr_x(i + 3, 0)
            htc(i + 2, 1)
            tr_x(i + 3, 1)
            wi2v(i + 2)
            if i - 1 < LAST:
                q_h2(i - 1)
            q_w3(i + 1)
            if i < LAST:
                s1a(i, 0)
                m1(i + 1, 0)
                s1a(i, 1)
                m1(i + 1, 1)
                s1a(i, 2)
                m1(i + 1, 2)
                s1a(i, 3)
                m1(i + 1, 3)
            if i - 1 < LAST:
                mm_mean(i - 1, 0)
                mm_mean(i - 1, 1)
            if i == LAST:
                for hf in range(2):
                    for tt in range(4):
                        s1a(i, tt, HALVES[hf])
                for hf in range(2):
                    for st in range(2):
                        nc.scalar.activation(
                            out=stT[:, st, HALVES[hf]], in_=t["pm", st][:, HALVES[hf]], func=ACT.Identity,
                            bias=kb[:, st : st + 1], scale=-1.0 / ACTIONS,
                        )
                for hf in range(2):
                    s1b(i, HALVES[hf])
                    q_h2(i, HALVES[hf])
                    mm_state(hf)
            w3copy(i + 2)
            wa3(i + 3)
            wi2s(i + 3)
            if i == -3:
                bias_prep_pe()
            q_pair(i + 2)
            if i == -2:
                bias_prep_v()

        def straight(a):
            return a in STRAIGHT

        def m2(a):
            if a >= ACTIONS:
                return
            for h in range(2):
                shape = [P, 2, S_OUT] if straight(a) else [P, BATCH]
                if a % 2 == 1 and h == 1:
                    ps2 = psum.tile(shape, F32, name="ps2", tag="pw", bufs=1)
                else:
                    ps2 = psum.tile(shape, F32, name="ps2", tag="ps1", bufs=3)
                t["ps2", a, h] = ps2
                if straight(a):
                    for bl in range(2):
                        rows = slice(P * (2 * h + bl), P * (2 * h + bl + 1))
                        nc.tensor.matmul_mx(
                            out=ps2[:, bl, :],
                            lhsT=h2q[:, a, rows].bitcast(FP8X4),
                            lhsT_scale=h2s[:, a, rows],
                            rhs=w3q[:, a, :].bitcast(FP8X4),
                            rhs_scale=w3s[:, a, :],
                            start=True,
                            stop=True,
                        )
                else:
                    mm2(ps2[:], a, h, True, True)

        def turn(src, tag):
            tiles = []
            for hb in range(2):
                pso = psum.tile([P, 2, S_OUT], F32, name="pso", tag=tag, bufs=2)
                for bl in range(2):
                    bt = 2 * hb + bl
                    for st in range(2):
                        nc.tensor.transpose(
                            pso[:, bl, P * st : P * (st + 1)], src[:, st, P * bt : P * (bt + 1)], ident_f[:]
                        )
                tiles.append(pso)
            return tiles

        m2(0)
        m2(1)
        for hf in range(2):
            nc.vector.tensor_tensor(
                out=baseT[:, :, HALVES[hf]], in0=t["pst", hf][:], in1=stT[:, :, HALVES[hf]], op=ALU.add
            )
        pbn = turn(baseT, "pt")
        for hb in range(2):
            nc.scalar.copy(out=baseN[:, 2 * hb : 2 * hb + 2, :], in_=pbn[hb][:])
        for g in range(len(STRAIGHT)):
            t2 = stream.tile([P, NB, S_OUT], F32, name="t2", tag="t2", bufs=2)
            nc.gpsimd.tensor_tensor(
                out=t2[:], in0=baseN[:], in1=b3b[:, g : g + 1, :].to_broadcast([P, NB, S_OUT]), op=ALU.add
            )
            t["t2", STRAIGHT[g]] = t2

        turned = 0
        for a in range(ACTIONS):
            if a % 2 == 0:
                if (a // 2) % 5 < 3:
                    stage = stream.tile([P, NB, 2, S_OUT], F32, name="stage", tag="stage", bufs=3)
                else:
                    stage = stream.tile([P, NB, 2, S_OUT], F32, name="stage", tag="pair", bufs=2, align_bytes=64)
            late = a >= ACTIONS - 2 or a < 2
            if straight(a):
                for hb in range(2):
                    nc.vector.tensor_tensor(
                        out=stage[:, 2 * hb : 2 * hb + 2, a % 2, :], in0=t["ps2", a, hb][:],
                        in1=t["t2", a][:, 2 * hb : 2 * hb + 2, :], op=ALU.add,
                    )
                m2(a + 2)
            else:
                advT = stream.tile([P, 2, BATCH], F32, name="advT", tag="advT", bufs=3)
                for st in range(2):
                    nc.vector.scalar_tensor_tensor(
                        out=advT[:, st, :], in0=t["ps2", a, st][:], scalar=b3T[:, st, a : a + 1],
                        in1=baseT[:, st, :], op0=ALU.add, op1=ALU.add,
                    )
                m2(a + 2)
                psos = turn(advT, "pm" if turned % 2 == 0 else "pt")
                turned += 1
                for hb in range(2):
                    nc.scalar.copy(out=stage[:, 2 * hb : 2 * hb + 2, a % 2, :], in_=psos[hb][:])
            if late:
                for hb in range(2):
                    nc.sync.dma_start(
                        out=out[2 * P * hb : 2 * P * (hb + 1), a, :].rearrange("(b n) s -> n b s", n=P),
                        in_=stage[:, 2 * hb : 2 * hb + 2, a % 2, :],
                    )
            elif a == ACTIONS - 3:
                held = stage
            elif a % 2 == 1:
                for hb in range(2):
                    nc.sync.dma_start(
                        out=out[2 * P * hb : 2 * P * (hb + 1), a - 1 : a + 1, :].rearrange("(b n) a s -> n b a s", n=P),
                        in_=stage[:, 2 * hb : 2 * hb + 2, :, :],
                    )
        for hb in range(2):
            nc.sync.dma_start(
                out=out[2 * P * hb : 2 * P * (hb + 1), ACTIONS - 4 : ACTIONS - 2, :].rearrange("(b n) a s -> n b a s", n=P),
                in_=held[:, 2 * hb : 2 * hb + 2, :, :],
            )
